import numpy as np
import ml_dtypes

BF16 = ml_dtypes.bfloat16


def bf(x):
    return np.asarray(x, np.float32).astype(BF16)


def f32(x):
    return np.asarray(x, np.float32)


def f64(x):
    return np.asarray(x).astype(np.float64)


def striped(idx):
    return np.tile(idx.reshape(-1, 16).T, (8, 1))


C, S, T, K, N = 128, 1024, 512, 4, 2048
EPS = 1e-5


def setup_inputs():
    return {"tok_emb": f32(np.random.standard_normal((C, S))), "pos_emb": f32(np.random.standard_normal((C, T))), "ln_gain": f32(1.0 + 0.1 * np.random.standard_normal((C, 1))), "ln_bias": f32(0.1 * np.random.standard_normal((C, 1))), "offs": striped(np.concatenate([np.random.permutation(S)[:T] for _ in range(K)]))}


def reference(tok_emb, pos_emb, ln_gain, ln_bias, offs):
    idx = offs[:16].T.reshape(-1)
    e = f64(tok_emb)[:, idx] + np.tile(f64(pos_emb), (1, K))
    mean = e.mean(axis=0, keepdims=True)
    var = ((e - mean) ** 2).mean(axis=0, keepdims=True)
    return (e - mean) / np.sqrt(var + EPS) * f64(ln_gain) + f64(ln_bias)

@@ -1,0 +1,82 @@
+import concourse.mybir as mybir
+
+F32 = mybir.dt.float32
+U16 = mybir.dt.uint16
+ALU = mybir.AluOpType
+ACT = mybir.ActivationFunctionType
+
+C = 128
+S = 1024
+T = 512
+K = 4
+N = K * T
+EPS = 1e-5
+
+FLOPS = 8 * C * N
+
+
+def tile_ternaryberttiny_kernel(tc, tok_emb, pos_emb, ln_gain, ln_bias, offs, out):
+    nc = tc.nc
+    with (
+        tc.tile_pool(name="held", bufs=1) as held,
+        tc.tile_pool(name="work", bufs=2) as work,
+        tc.psum_pool(name="centred_banks", bufs=4) as centred_banks,
+        tc.psum_pool(name="variance_banks", bufs=2) as variance_banks,
+    ):
+        offsets = held.tile([C, N // 16], U16, name="offsets")
+        nc.sync.dma_start(offsets[:], offs)
+        table = held.tile([C, S], F32, name="table")
+        nc.sync.dma_start(table[:], tok_emb)
+        positions = held.tile([C, T], F32, name="positions")
+        nc.scalar.dma_start(positions[:], pos_emb)
+        gain = held.tile([C, 1], F32, name="gain")
+        nc.gpsimd.dma_start(gain[:], ln_gain)
+        bias = held.tile([C, 1], F32, name="bias")
+        nc.gpsimd.dma_start(bias[:], ln_bias)
+
+        centre_w = held.tile([C, C], F32, name="centre_w")
+        nc.gpsimd.memset(centre_w[:], -1.0 / C)
+        nc.gpsimd.affine_select(
+            out=centre_w[:],
+            in_=centre_w[:],
+            pattern=[[-1, C]],
+            compare_op=ALU.not_equal,
+            fill=1.0 - 1.0 / C,
+            base=0,
+            channel_multiplier=1,
+        )
+        mean_w = held.tile([C, C], F32, name="mean_w")
+        nc.vector.memset(mean_w[:], 1.0 / C)
+        eps = held.tile([C, 1], F32, name="eps")
+        nc.vector.memset(eps[:], EPS)
+
+        embedded = [held.tile([C, T], F32, name=f"embedded{k}") for k in range(K)]
+        for k in range(K):
+            words = table[:].indirect(offsets[:, k * (T // 16) : (k + 1) * (T // 16)])
+            nc.vector.tensor_tensor(embedded[k][:], words, positions[:], ALU.add)
+
+        centred = {}
+        squares = {}
+
+        def centre_and_square(k):
+            centred[k] = centred_banks.tile([C, T], F32, name="centred")
+            nc.tensor.matmul(centred[k][:], centre_w[:], embedded[k][:], start=True, stop=True)
+            squares[k] = work.tile([C, T], F32, name="squares")
+            nc.scalar.activation(squares[k][:], centred[k][:], ACT.Square)
+
+        def normalise_and_store(k):
+            variance = variance_banks.tile([C, T], F32, name="variance")
+            nc.tensor.matmul(variance[:], mean_w[:], squares[k][:], start=True, stop=True)
+            rstd = work.tile([C, T], F32, name="rstd")
+            nc.scalar.activation(rstd[:], variance[:], ACT.Abs_reciprocal_sqrt, bias=eps[:])
+            normed = work.tile([C, T], F32, name="normed")
+            nc.vector.tensor_tensor(normed[:], centred[k][:], rstd[:], ALU.mult)
+            result = work.tile([C, T], F32, name="result")
+            nc.scalar.activation(result[:], normed[:], ACT.Identity, bias=bias[:], scale=gain[:])
+            nc.sync.dma_start(out[:, k * T : (k + 1) * T], result[:])
+
+        centre_and_square(0)
+        for k in range(K):
+            if k + 1 < K:
+                centre_and_square(k + 1)
+            normalise_and_store(k)

@@ -11,6 +11,7 @@ T = 512
 K = 4
 N = K * T
 EPS = 1e-5
+WARM_UP = 7
 
 FLOPS = 8 * C * N
 
@@ -22,17 +23,18 @@ def tile_ternaryberttiny_kernel(tc, tok_emb, pos_emb, ln_gain, ln_bias, offs, ou
         tc.tile_pool(name="work", bufs=2) as work,
         tc.psum_pool(name="centred_banks", bufs=4) as centred_banks,
         tc.psum_pool(name="variance_banks", bufs=2) as variance_banks,
+        tc.psum_pool(name="warm_bank", bufs=1) as warm_bank,
     ):
         offsets = held.tile([C, N // 16], U16, name="offsets")
         nc.sync.dma_start(offsets[:], offs)
         table = held.tile([C, S], F32, name="table")
-        nc.sync.dma_start(table[:], tok_emb)
+        nc.scalar.dma_start(table[:], tok_emb)
         positions = held.tile([C, T], F32, name="positions")
-        nc.scalar.dma_start(positions[:], pos_emb)
+        nc.sync.dma_start(positions[:], pos_emb)
         gain = held.tile([C, 1], F32, name="gain")
-        nc.gpsimd.dma_start(gain[:], ln_gain)
+        nc.sync.dma_start(gain[:], ln_gain)
         bias = held.tile([C, 1], F32, name="bias")
-        nc.gpsimd.dma_start(bias[:], ln_bias)
+        nc.sync.dma_start(bias[:], ln_bias)
 
         centre_w = held.tile([C, C], F32, name="centre_w")
         nc.gpsimd.memset(centre_w[:], -1.0 / C)
@@ -49,6 +51,10 @@ def tile_ternaryberttiny_kernel(tc, tok_emb, pos_emb, ln_gain, ln_bias, offs, ou
         nc.vector.memset(mean_w[:], 1.0 / C)
         eps = held.tile([C, 1], F32, name="eps")
         nc.vector.memset(eps[:], EPS)
+
+        warm = warm_bank.tile([C, C], F32, name="warm")
+        for i in range(WARM_UP):
+            nc.tensor.matmul(warm[:], mean_w[:], mean_w[:], start=True, stop=True)
 
         embedded = [held.tile([C, T], F32, name=f"embedded{k}") for k in range(K)]
         for k in range(K):

@@ -11,7 +11,6 @@ T = 512
 K = 4
 N = K * T
 EPS = 1e-5
-WARM_UP = 7
 
 FLOPS = 8 * C * N
 
@@ -23,7 +22,6 @@ def tile_ternaryberttiny_kernel(tc, tok_emb, pos_emb, ln_gain, ln_bias, offs, ou
         tc.tile_pool(name="work", bufs=2) as work,
         tc.psum_pool(name="centred_banks", bufs=4) as centred_banks,
         tc.psum_pool(name="variance_banks", bufs=2) as variance_banks,
-        tc.psum_pool(name="warm_bank", bufs=1) as warm_bank,
     ):
         offsets = held.tile([C, N // 16], U16, name="offsets")
         nc.sync.dma_start(offsets[:], offs)
@@ -51,10 +49,6 @@ def tile_ternaryberttiny_kernel(tc, tok_emb, pos_emb, ln_gain, ln_bias, offs, ou
         nc.vector.memset(mean_w[:], 1.0 / C)
         eps = held.tile([C, 1], F32, name="eps")
         nc.vector.memset(eps[:], EPS)
-
-        warm = warm_bank.tile([C, C], F32, name="warm")
-        for i in range(WARM_UP):
-            nc.tensor.matmul(warm[:], mean_w[:], mean_w[:], start=True, stop=True)
 
         embedded = [held.tile([C, T], F32, name=f"embedded{k}") for k in range(K)]
         for k in range(K):

@@ -11,6 +11,7 @@ T = 512
 K = 4
 N = K * T
 EPS = 1e-5
+WARM_UP = 7
 
 FLOPS = 8 * C * N
 
@@ -22,6 +23,7 @@ def tile_ternaryberttiny_kernel(tc, tok_emb, pos_emb, ln_gain, ln_bias, offs, ou
         tc.tile_pool(name="work", bufs=2) as work,
         tc.psum_pool(name="centred_banks", bufs=4) as centred_banks,
         tc.psum_pool(name="variance_banks", bufs=2) as variance_banks,
+        tc.psum_pool(name="warm_bank", bufs=1) as warm_bank,
     ):
         offsets = held.tile([C, N // 16], U16, name="offsets")
         nc.sync.dma_start(offsets[:], offs)
@@ -50,6 +52,10 @@ def tile_ternaryberttiny_kernel(tc, tok_emb, pos_emb, ln_gain, ln_bias, offs, ou
         eps = held.tile([C, 1], F32, name="eps")
         nc.vector.memset(eps[:], EPS)
 
+        warm = warm_bank.tile([C, C], F32, name="warm")
+        for i in range(WARM_UP):
+            nc.tensor.matmul(warm[:], mean_w[:], mean_w[:], start=True, stop=True)
+
         embedded = [held.tile([C, T], F32, name=f"embedded{k}") for k in range(K)]
         for k in range(K):
             words = table[:].indirect(offsets[:, k * (T // 16) : (k + 1) * (T // 16)])
@@ -72,7 +78,7 @@ def tile_ternaryberttiny_kernel(tc, tok_emb, pos_emb, ln_gain, ln_bias, offs, ou
             normed = work.tile([C, T], F32, name="normed")
             nc.vector.tensor_tensor(normed[:], centred[k][:], rstd[:], ALU.mult)
             result = work.tile([C, T], F32, name="result")
-            nc.scalar.activation(result[:], normed[:], ACT.Identity, bias=bias[:], scale=gain[:])
+            nc.vector.tensor_scalar(result[:], normed[:], gain[:], bias[:], ALU.mult, ALU.add)
             nc.sync.dma_start(out[:, k * T : (k + 1) * T], result[:])
 
         centre_and_square(0)

@@ -8,8 +8,9 @@ ACT = mybir.ActivationFunctionType
 C = 128
 S = 1024
 T = 512
-K = 4
-N = K * T
+N = 4 * T
+W = 256
+PIECES = N // W
 EPS = 1e-5
 WARM_UP = 7
 
@@ -20,8 +21,8 @@ def tile_ternaryberttiny_kernel(tc, tok_emb, pos_emb, ln_gain, ln_bias, offs, ou
     nc = tc.nc
     with (
         tc.tile_pool(name="held", bufs=1) as held,
-        tc.tile_pool(name="work", bufs=2) as work,
-        tc.psum_pool(name="centred_banks", bufs=4) as centred_banks,
+        tc.tile_pool(name="work", bufs=3) as work,
+        tc.psum_pool(name="centred_banks", bufs=5) as centred_banks,
         tc.psum_pool(name="variance_banks", bufs=2) as variance_banks,
         tc.psum_pool(name="warm_bank", bufs=1) as warm_bank,
     ):
@@ -31,10 +32,6 @@ def tile_ternaryberttiny_kernel(tc, tok_emb, pos_emb, ln_gain, ln_bias, offs, ou
         nc.scalar.dma_start(table[:], tok_emb)
         positions = held.tile([C, T], F32, name="positions")
         nc.sync.dma_start(positions[:], pos_emb)
-        gain = held.tile([C, 1], F32, name="gain")
-        nc.sync.dma_start(gain[:], ln_gain)
-        bias = held.tile([C, 1], F32, name="bias")
-        nc.sync.dma_start(bias[:], ln_bias)
 
         centre_w = held.tile([C, C], F32, name="centre_w")
         nc.gpsimd.memset(centre_w[:], -1.0 / C)
@@ -47,6 +44,10 @@ def tile_ternaryberttiny_kernel(tc, tok_emb, pos_emb, ln_gain, ln_bias, offs, ou
             base=0,
             channel_multiplier=1,
         )
+        gain = held.tile([C, 1], F32, name="gain")
+        nc.gpsimd.dma_start(gain[:], ln_gain)
+        bias = held.tile([C, 1], F32, name="bias")
+        nc.gpsimd.dma_start(bias[:], ln_bias)
         mean_w = held.tile([C, C], F32, name="mean_w")
         nc.vector.memset(mean_w[:], 1.0 / C)
         eps = held.tile([C, 1], F32, name="eps")
@@ -56,33 +57,34 @@ def tile_ternaryberttiny_kernel(tc, tok_emb, pos_emb, ln_gain, ln_bias, offs, ou
         for i in range(WARM_UP):
             nc.tensor.matmul(warm[:], mean_w[:], mean_w[:], start=True, stop=True)
 
-        embedded = [held.tile([C, T], F32, name=f"embedded{k}") for k in range(K)]
-        for k in range(K):
-            words = table[:].indirect(offsets[:, k * (T // 16) : (k + 1) * (T // 16)])
-            nc.vector.tensor_tensor(embedded[k][:], words, positions[:], ALU.add)
+        embedded = [held.tile([C, W], F32, name=f"embedded{p}") for p in range(PIECES)]
+        for p in range(PIECES):
+            words = table[:].indirect(offsets[:, p * (W // 16) : (p + 1) * (W // 16)])
+            first = (p * W) % T
+            nc.vector.tensor_tensor(embedded[p][:], words, positions[:, first : first + W], ALU.add)
 
         centred = {}
         squares = {}
 
-        def centre_and_square(k):
-            centred[k] = centred_banks.tile([C, T], F32, name="centred")
-            nc.tensor.matmul(centred[k][:], centre_w[:], embedded[k][:], start=True, stop=True)
-            squares[k] = work.tile([C, T], F32, name="squares")
-            nc.scalar.activation(squares[k][:], centred[k][:], ACT.Square)
+        def centre_and_square(p):
+            centred[p] = centred_banks.tile([C, W], F32, name="centred")
+            nc.tensor.matmul(centred[p][:], centre_w[:], embedded[p][:], start=True, stop=True)
+            squares[p] = work.tile([C, W], F32, name="squares")
+            nc.scalar.activation(squares[p][:], centred[p][:], ACT.Square)
 
-        def normalise_and_store(k):
-            variance = variance_banks.tile([C, T], F32, name="variance")
-            nc.tensor.matmul(variance[:], mean_w[:], squares[k][:], start=True, stop=True)
-            rstd = work.tile([C, T], F32, name="rstd")
+        def normalise_and_store(p):
+            variance = variance_banks.tile([C, W], F32, name="variance")
+            nc.tensor.matmul(variance[:], mean_w[:], squares[p][:], start=True, stop=True)
+            rstd = work.tile([C, W], F32, name="rstd")
             nc.scalar.activation(rstd[:], variance[:], ACT.Abs_reciprocal_sqrt, bias=eps[:])
-            normed = work.tile([C, T], F32, name="normed")
-            nc.vector.tensor_tensor(normed[:], centred[k][:], rstd[:], ALU.mult)
-            result = work.tile([C, T], F32, name="result")
+            normed = work.tile([C, W], F32, name="normed")
+            nc.vector.tensor_tensor(normed[:], centred[p][:], rstd[:], ALU.mult)
+            result = work.tile([C, W], F32, name="result")
             nc.vector.tensor_scalar(result[:], normed[:], gain[:], bias[:], ALU.mult, ALU.add)
-            nc.sync.dma_start(out[:, k * T : (k + 1) * T], result[:])
+            nc.sync.dma_start(out[:, p * W : (p + 1) * W], result[:])
 
         centre_and_square(0)
-        for k in range(K):
-            if k + 1 < K:
-                centre_and_square(k + 1)
-            normalise_and_store(k)
+        for p in range(PIECES):
+            if p + 1 < PIECES:
+                centre_and_square(p + 1)
+            normalise_and_store(p)

@@ -21,10 +21,8 @@ def tile_ternaryberttiny_kernel(tc, tok_emb, pos_emb, ln_gain, ln_bias, offs, ou
     nc = tc.nc
     with (
         tc.tile_pool(name="held", bufs=1) as held,
-        tc.tile_pool(name="work", bufs=3) as work,
-        tc.psum_pool(name="centred_banks", bufs=5) as centred_banks,
-        tc.psum_pool(name="variance_banks", bufs=2) as variance_banks,
-        tc.psum_pool(name="warm_bank", bufs=1) as warm_bank,
+        tc.tile_pool(name="work", bufs=PIECES) as work,
+        tc.psum_pool(name="psum", bufs=1) as psum,
     ):
         offsets = held.tile([C, N // 16], U16, name="offsets")
         nc.sync.dma_start(offsets[:], offs)
@@ -53,9 +51,9 @@ def tile_ternaryberttiny_kernel(tc, tok_emb, pos_emb, ln_gain, ln_bias, offs, ou
         eps = held.tile([C, 1], F32, name="eps")
         nc.vector.memset(eps[:], EPS)
 
-        warm = warm_bank.tile([C, C], F32, name="warm")
+        banks = [psum.tile([C, 2 * W], F32, name=f"bank{p}") for p in range(PIECES)]
         for i in range(WARM_UP):
-            nc.tensor.matmul(warm[:], mean_w[:], mean_w[:], start=True, stop=True)
+            nc.tensor.matmul(banks[PIECES - 1][:, 0:C], mean_w[:], mean_w[:], start=True, stop=True)
 
         embedded = [held.tile([C, W], F32, name=f"embedded{p}") for p in range(PIECES)]
         for p in range(PIECES):
@@ -63,22 +61,22 @@ def tile_ternaryberttiny_kernel(tc, tok_emb, pos_emb, ln_gain, ln_bias, offs, ou
             first = (p * W) % T
             nc.vector.tensor_tensor(embedded[p][:], words, positions[:, first : first + W], ALU.add)
 
-        centred = {}
         squares = {}
 
         def centre_and_square(p):
-            centred[p] = centred_banks.tile([C, W], F32, name="centred")
-            nc.tensor.matmul(centred[p][:], centre_w[:], embedded[p][:], start=True, stop=True)
+            centred = banks[p][:, 0:W]
+            nc.tensor.matmul(centred, centre_w[:], embedded[p][:], start=True, stop=True)
             squares[p] = work.tile([C, W], F32, name="squares")
-            nc.scalar.activation(squares[p][:], centred[p][:], ACT.Square)
+            nc.scalar.activation(squares[p][:], centred, ACT.Square)
 
         def normalise_and_store(p):
-            variance = variance_banks.tile([C, W], F32, name="variance")
-            nc.tensor.matmul(variance[:], mean_w[:], squares[p][:], start=True, stop=True)
+            centred = banks[p][:, 0:W]
+            variance = banks[p][:, W : 2 * W]
+            nc.tensor.matmul(variance, mean_w[:], squares[p][:], start=True, stop=True)
             rstd = work.tile([C, W], F32, name="rstd")
-            nc.scalar.activation(rstd[:], variance[:], ACT.Abs_reciprocal_sqrt, bias=eps[:])
+            nc.scalar.activation(rstd[:], variance, ACT.Abs_reciprocal_sqrt, bias=eps[:])
             normed = work.tile([C, W], F32, name="normed")
-            nc.vector.tensor_tensor(normed[:], centred[p][:], rstd[:], ALU.mult)
+            nc.vector.tensor_tensor(normed[:], centred, rstd[:], ALU.mult)
             result = work.tile([C, W], F32, name="result")
             nc.vector.tensor_scalar(result[:], normed[:], gain[:], bias[:], ALU.mult, ALU.add)
             nc.sync.dma_start(out[:, p * W : (p + 1) * W], result[:])

@@ -13,6 +13,7 @@ W = 256
 PIECES = N // W
 EPS = 1e-5
 WARM_UP = 7
+AHEAD = 2
 
 FLOPS = 8 * C * N
 
@@ -30,6 +31,10 @@ def tile_ternaryberttiny_kernel(tc, tok_emb, pos_emb, ln_gain, ln_bias, offs, ou
         nc.scalar.dma_start(table[:], tok_emb)
         positions = held.tile([C, T], F32, name="positions")
         nc.sync.dma_start(positions[:], pos_emb)
+        gain = held.tile([C, 1], F32, name="gain")
+        nc.sync.dma_start(gain[:], ln_gain)
+        bias = held.tile([C, 1], F32, name="bias")
+        nc.sync.dma_start(bias[:], ln_bias)
 
         centre_w = held.tile([C, C], F32, name="centre_w")
         nc.gpsimd.memset(centre_w[:], -1.0 / C)
@@ -42,10 +47,6 @@ def tile_ternaryberttiny_kernel(tc, tok_emb, pos_emb, ln_gain, ln_bias, offs, ou
             base=0,
             channel_multiplier=1,
         )
-        gain = held.tile([C, 1], F32, name="gain")
-        nc.gpsimd.dma_start(gain[:], ln_gain)
-        bias = held.tile([C, 1], F32, name="bias")
-        nc.gpsimd.dma_start(bias[:], ln_bias)
         mean_w = held.tile([C, C], F32, name="mean_w")
         nc.vector.memset(mean_w[:], 1.0 / C)
         eps = held.tile([C, 1], F32, name="eps")
@@ -81,8 +82,9 @@ def tile_ternaryberttiny_kernel(tc, tok_emb, pos_emb, ln_gain, ln_bias, offs, ou
             nc.vector.tensor_scalar(result[:], normed[:], gain[:], bias[:], ALU.mult, ALU.add)
             nc.sync.dma_start(out[:, p * W : (p + 1) * W], result[:])
 
-        centre_and_square(0)
+        for p in range(AHEAD):
+            centre_and_square(p)
         for p in range(PIECES):
-            if p + 1 < PIECES:
-                centre_and_square(p + 1)
+            if p + AHEAD < PIECES:
+                centre_and_square(p + AHEAD)
             normalise_and_store(p)

@@ -79,7 +79,8 @@ def tile_ternaryberttiny_kernel(tc, tok_emb, pos_emb, ln_gain, ln_bias, offs, ou
             normed = work.tile([C, W], F32, name="normed")
             nc.vector.tensor_tensor(normed[:], centred, rstd[:], ALU.mult)
             result = work.tile([C, W], F32, name="result")
-            nc.vector.tensor_scalar(result[:], normed[:], gain[:], bias[:], ALU.mult, ALU.add)
+            engine = nc.gpsimd if p % 2 == 0 else nc.vector
+            engine.tensor_scalar(result[:], normed[:], gain[:], bias[:], ALU.mult, ALU.add)
             nc.sync.dma_start(out[:, p * W : (p + 1) * W], result[:])
 
         for p in range(AHEAD):

@@ -10,10 +10,14 @@ S = 1024
 T = 512
 N = 4 * T
 W = 256
-PIECES = N // W
+BANKS = 8
+WIDTHS = [W] * (N // W - 1) + [W // 2] * 2
+STARTS = [sum(WIDTHS[:p]) for p in range(len(WIDTHS))]
+PIECES = len(WIDTHS)
 EPS = 1e-5
 WARM_UP = 7
 AHEAD = 2
+HELPED = 5
 
 FLOPS = 8 * C * N
 
@@ -52,36 +56,41 @@ def tile_ternaryberttiny_kernel(tc, tok_emb, pos_emb, ln_gain, ln_bias, offs, ou
         eps = held.tile([C, 1], F32, name="eps")
         nc.vector.memset(eps[:], EPS)
 
-        banks = [psum.tile([C, 2 * W], F32, name=f"bank{p}") for p in range(PIECES)]
-        for i in range(WARM_UP):
-            nc.tensor.matmul(banks[PIECES - 1][:, 0:C], mean_w[:], mean_w[:], start=True, stop=True)
+        banks = [psum.tile([C, 2 * W], F32, name=f"bank{b}") for b in range(BANKS)]
 
-        embedded = [held.tile([C, W], F32, name=f"embedded{p}") for p in range(PIECES)]
+        for i in range(WARM_UP):
+            nc.tensor.matmul(banks[BANKS - 1][:, 0:C], mean_w[:], mean_w[:], start=True, stop=True)
+
+        embedded = []
         for p in range(PIECES):
-            words = table[:].indirect(offsets[:, p * (W // 16) : (p + 1) * (W // 16)])
-            first = (p * W) % T
-            nc.vector.tensor_tensor(embedded[p][:], words, positions[:, first : first + W], ALU.add)
+            start, width = STARTS[p], WIDTHS[p]
+            words = table[:].indirect(offsets[:, start // 16 : (start + width) // 16])
+            embedded.append(held.tile([C, width], F32, name=f"embedded{p}"))
+            first = start % T
+            nc.vector.tensor_tensor(embedded[p][:], words, positions[:, first : first + width], ALU.add)
 
         squares = {}
 
         def centre_and_square(p):
-            centred = banks[p][:, 0:W]
+            width = WIDTHS[p]
+            centred = banks[p % BANKS][:, 0:width]
             nc.tensor.matmul(centred, centre_w[:], embedded[p][:], start=True, stop=True)
             squares[p] = work.tile([C, W], F32, name="squares")
-            nc.scalar.activation(squares[p][:], centred, ACT.Square)
+            nc.scalar.activation(squares[p][:, 0:width], centred, ACT.Square)
 
         def normalise_and_store(p):
-            centred = banks[p][:, 0:W]
-            variance = banks[p][:, W : 2 * W]
-            nc.tensor.matmul(variance, mean_w[:], squares[p][:], start=True, stop=True)
+            start, width = STARTS[p], WIDTHS[p]
+            centred = banks[p % BANKS][:, 0:width]
+            variance = banks[p % BANKS][:, W : W + width]
+            nc.tensor.matmul(variance, mean_w[:], squares[p][:, 0:width], start=True, stop=True)
             rstd = work.tile([C, W], F32, name="rstd")
-            nc.scalar.activation(rstd[:], variance, ACT.Abs_reciprocal_sqrt, bias=eps[:])
+            nc.scalar.activation(rstd[:, 0:width], variance, ACT.Abs_reciprocal_sqrt, bias=eps[:])
             normed = work.tile([C, W], F32, name="normed")
-            nc.vector.tensor_tensor(normed[:], centred, rstd[:], ALU.mult)
+            nc.vector.tensor_tensor(normed[:, 0:width], centred, rstd[:, 0:width], ALU.mult)
             result = work.tile([C, W], F32, name="result")
-            engine = nc.gpsimd if p % 2 == 0 else nc.vector
-            engine.tensor_scalar(result[:], normed[:], gain[:], bias[:], ALU.mult, ALU.add)
-            nc.sync.dma_start(out[:, p * W : (p + 1) * W], result[:])
+            engine = nc.gpsimd if p < HELPED else nc.vector
+            engine.tensor_scalar(result[:, 0:width], normed[:, 0:width], gain[:], bias[:], ALU.mult, ALU.add)
+            nc.sync.dma_start(out[:, start : start + width], result[:, 0:width])
 
         for p in range(AHEAD):
             centre_and_square(p)

@@ -11,13 +11,13 @@ T = 512
 N = 4 * T
 W = 256
 BANKS = 8
-WIDTHS = [W] * (N // W - 1) + [W // 2] * 2
+WIDTHS = [W // 2] * 2 + [W] * (N // W - 2) + [W // 2] * 2
 STARTS = [sum(WIDTHS[:p]) for p in range(len(WIDTHS))]
 PIECES = len(WIDTHS)
 EPS = 1e-5
 WARM_UP = 7
 AHEAD = 2
-HELPED = 5
+HELPED = 6
 
 FLOPS = 8 * C * N
 

@@ -31,10 +31,13 @@ def tile_ternaryberttiny_kernel(tc, tok_emb, pos_emb, ln_gain, ln_bias, offs, ou
     ):
         offsets = held.tile([C, N // 16], U16, name="offsets")
         nc.sync.dma_start(offsets[:], offs)
+        early = WIDTHS[0]
+        first_positions = held.tile([C, early], F32, name="first_positions")
+        nc.sync.dma_start(first_positions[:], pos_emb[:, 0:early])
         table = held.tile([C, S], F32, name="table")
         nc.scalar.dma_start(table[:], tok_emb)
         positions = held.tile([C, T], F32, name="positions")
-        nc.sync.dma_start(positions[:], pos_emb)
+        nc.scalar.dma_start(positions[:], pos_emb)
         gain = held.tile([C, 1], F32, name="gain")
         nc.sync.dma_start(gain[:], ln_gain)
         bias = held.tile([C, 1], F32, name="bias")
@@ -67,7 +70,8 @@ def tile_ternaryberttiny_kernel(tc, tok_emb, pos_emb, ln_gain, ln_bias, offs, ou
             words = table[:].indirect(offsets[:, start // 16 : (start + width) // 16])
             embedded.append(held.tile([C, width], F32, name=f"embedded{p}"))
             first = start % T
-            nc.vector.tensor_tensor(embedded[p][:], words, positions[:, first : first + width], ALU.add)
+            added = first_positions[:] if p == 0 else positions[:, first : first + width]
+            nc.vector.tensor_tensor(embedded[p][:], words, added, ALU.add)
 
         squares = {}
 

@@ -1,4 +1,5 @@
 import concourse.mybir as mybir
+from concourse.masks import make_identity
 
 F32 = mybir.dt.float32
 U16 = mybir.dt.uint16
@@ -9,15 +10,14 @@ C = 128
 S = 1024
 T = 512
 N = 4 * T
-W = 256
+B = 128
+W = 2 * B
 BANKS = 8
-WIDTHS = [W // 2] * 2 + [W] * (N // W - 2) + [W // 2] * 2
+WIDTHS = [B] * 2 + [W] * (N // W - 2) + [B] * 2
 STARTS = [sum(WIDTHS[:p]) for p in range(len(WIDTHS))]
 PIECES = len(WIDTHS)
 EPS = 1e-5
 WARM_UP = 7
-AHEAD = 2
-HELPED = 6
 
 FLOPS = 8 * C * N
 
@@ -54,15 +54,17 @@ def tile_ternaryberttiny_kernel(tc, tok_emb, pos_emb, ln_gain, ln_bias, offs, ou
             base=0,
             channel_multiplier=1,
         )
-        mean_w = held.tile([C, C], F32, name="mean_w")
-        nc.vector.memset(mean_w[:], 1.0 / C)
-        eps = held.tile([C, 1], F32, name="eps")
+        identity = held.tile([C, C], F32, name="identity")
+        make_identity(nc, identity[:])
+        eps = held.tile([B, 1], F32, name="eps")
         nc.vector.memset(eps[:], EPS)
+        warm = held.tile([C, C], F32, name="warm")
+        nc.vector.memset(warm[:], 0.0)
 
         banks = [psum.tile([C, 2 * W], F32, name=f"bank{b}") for b in range(BANKS)]
 
         for i in range(WARM_UP):
-            nc.tensor.matmul(banks[BANKS - 1][:, 0:C], mean_w[:], mean_w[:], start=True, stop=True)
+            nc.tensor.matmul(banks[BANKS - 1][:, 0:C], warm[:], warm[:], start=True, stop=True)
 
         embedded = []
         for p in range(PIECES):
@@ -73,32 +75,34 @@ def tile_ternaryberttiny_kernel(tc, tok_emb, pos_emb, ln_gain, ln_bias, offs, ou
             added = first_positions[:] if p == 0 else positions[:, first : first + width]
             nc.vector.tensor_tensor(embedded[p][:], words, added, ALU.add)
 
-        squares = {}
-
-        def centre_and_square(p):
-            width = WIDTHS[p]
-            centred = banks[p % BANKS][:, 0:width]
-            nc.tensor.matmul(centred, centre_w[:], embedded[p][:], start=True, stop=True)
-            squares[p] = work.tile([C, W], F32, name="squares")
-            nc.scalar.activation(squares[p][:, 0:width], centred, ACT.Square)
-
-        def normalise_and_store(p):
-            start, width = STARTS[p], WIDTHS[p]
-            centred = banks[p % BANKS][:, 0:width]
-            variance = banks[p % BANKS][:, W : W + width]
-            nc.tensor.matmul(variance, mean_w[:], squares[p][:, 0:width], start=True, stop=True)
-            rstd = work.tile([C, W], F32, name="rstd")
-            nc.scalar.activation(rstd[:, 0:width], variance, ACT.Abs_reciprocal_sqrt, bias=eps[:])
-            normed = work.tile([C, W], F32, name="normed")
-            nc.vector.tensor_tensor(normed[:, 0:width], centred, rstd[:, 0:width], ALU.mult)
-            result = work.tile([C, W], F32, name="result")
-            engine = nc.gpsimd if p < HELPED else nc.vector
-            engine.tensor_scalar(result[:, 0:width], normed[:, 0:width], gain[:], bias[:], ALU.mult, ALU.add)
-            nc.sync.dma_start(out[:, start : start + width], result[:, 0:width])
-
-        for p in range(AHEAD):
-            centre_and_square(p)
         for p in range(PIECES):
-            if p + AHEAD < PIECES:
-                centre_and_square(p + AHEAD)
-            normalise_and_store(p)
+            start, width = STARTS[p], WIDTHS[p]
+            blocks = width // B
+            centred = banks[p % BANKS][:, 0:width]
+            turned_back = banks[p % BANKS][:, W : W + width]
+
+            sums = work.tile([B, W // B], F32, name="sums")
+            for b in range(blocks):
+                cols = slice(b * B, (b + 1) * B)
+                nc.tensor.matmul(centred[:, cols], embedded[p][:, cols], centre_w[:], start=True, stop=True)
+            for b in range(blocks):
+                squares = work.tile([B, C], F32, name="squares")
+                cols = slice(b * B, (b + 1) * B)
+                nc.scalar.activation(squares[:], centred[:, cols], ACT.Square, accum_out=sums[:, b : b + 1])
+            rstd = work.tile([B, W // B], F32, name="rstd")
+            nc.scalar.activation(
+                rstd[:, 0:blocks], sums[:, 0:blocks], ACT.Abs_reciprocal_sqrt, bias=eps[:], scale=1.0 / C
+            )
+            normed = work.tile([B, W], F32, name="normed")
+            nc.vector.tensor_tensor(
+                normed[:, 0:width].rearrange("p (b c) -> p b c", c=C),
+                centred.rearrange("p (b c) -> p b c", c=C),
+                rstd[:, 0:blocks].unsqueeze(2).to_broadcast([B, blocks, C]),
+                ALU.mult,
+            )
+            for b in range(blocks):
+                cols = slice(b * B, (b + 1) * B)
+                nc.tensor.transpose(turned_back[:, cols], normed[:, cols], identity[:])
+            result = work.tile([C, W], F32, name="result")
+            nc.scalar.activation(result[:, 0:width], turned_back, ACT.Identity, bias=bias[:], scale=gain[:])
+            nc.sync.dma_start(out[:, start : start + width], result[:, 0:width])

@@ -12,10 +12,9 @@ T = 512
 N = 4 * T
 B = 128
 W = 2 * B
-BANKS = 8
-WIDTHS = [B] * 2 + [W] * (N // W - 2) + [B] * 2
-STARTS = [sum(WIDTHS[:p]) for p in range(len(WIDTHS))]
-PIECES = len(WIDTHS)
+BANK = 2 * W
+PIECES = N // W
+LOOK_UPS = [B] * 2 + [W] * (PIECES - 1)
 EPS = 1e-5
 WARM_UP = 7
 
@@ -31,7 +30,7 @@ def tile_ternaryberttiny_kernel(tc, tok_emb, pos_emb, ln_gain, ln_bias, offs, ou
     ):
         offsets = held.tile([C, N // 16], U16, name="offsets")
         nc.sync.dma_start(offsets[:], offs)
-        early = WIDTHS[0]
+        early = LOOK_UPS[0]
         first_positions = held.tile([C, early], F32, name="first_positions")
         nc.sync.dma_start(first_positions[:], pos_emb[:, 0:early])
         table = held.tile([C, S], F32, name="table")
@@ -61,48 +60,45 @@ def tile_ternaryberttiny_kernel(tc, tok_emb, pos_emb, ln_gain, ln_bias, offs, ou
         warm = held.tile([C, C], F32, name="warm")
         nc.vector.memset(warm[:], 0.0)
 
-        banks = [psum.tile([C, 2 * W], F32, name=f"bank{b}") for b in range(BANKS)]
+        banks = [psum.tile([C, BANK], F32, name=f"bank{p}") for p in range(PIECES)]
 
         for i in range(WARM_UP):
-            nc.tensor.matmul(banks[BANKS - 1][:, 0:C], warm[:], warm[:], start=True, stop=True)
+            nc.tensor.matmul(banks[PIECES - 1][:, 0:C], warm[:], warm[:], start=True, stop=True)
 
-        embedded = []
-        for p in range(PIECES):
-            start, width = STARTS[p], WIDTHS[p]
+        embedded = held.tile([C, N], F32, name="embedded")
+        start = 0
+        for k, width in enumerate(LOOK_UPS):
             words = table[:].indirect(offsets[:, start // 16 : (start + width) // 16])
-            embedded.append(held.tile([C, width], F32, name=f"embedded{p}"))
             first = start % T
-            added = first_positions[:] if p == 0 else positions[:, first : first + width]
-            nc.vector.tensor_tensor(embedded[p][:], words, added, ALU.add)
+            added = first_positions[:] if k == 0 else positions[:, first : first + width]
+            nc.vector.tensor_tensor(embedded[:, start : start + width], words, added, ALU.add)
+            start += width
+
+        blocks = [slice(b * B, (b + 1) * B) for b in range(W // B)]
+        rstds = []
+        for p in range(PIECES):
+            centred = banks[p][:, 0:W]
+            for cols in blocks:
+                block = embedded[:, p * W + cols.start : p * W + cols.stop]
+                nc.tensor.matmul(centred[:, cols], block, centre_w[:], start=True, stop=True)
+            sums = work.tile([B, W // B], F32, name="sums")
+            for b, cols in enumerate(blocks):
+                squares = work.tile([B, C], F32, name="squares")
+                nc.scalar.activation(squares[:], centred[:, cols], ACT.Square, accum_out=sums[:, b : b + 1])
+            rstds.append(held.tile([B, W // B], F32, name=f"rstd{p}"))
+            nc.scalar.activation(rstds[p][:], sums[:], ACT.Abs_reciprocal_sqrt, bias=eps[:], scale=1.0 / C)
 
         for p in range(PIECES):
-            start, width = STARTS[p], WIDTHS[p]
-            blocks = width // B
-            centred = banks[p % BANKS][:, 0:width]
-            turned_back = banks[p % BANKS][:, W : W + width]
-
-            sums = work.tile([B, W // B], F32, name="sums")
-            for b in range(blocks):
-                cols = slice(b * B, (b + 1) * B)
-                nc.tensor.matmul(centred[:, cols], embedded[p][:, cols], centre_w[:], start=True, stop=True)
-            for b in range(blocks):
-                squares = work.tile([B, C], F32, name="squares")
-                cols = slice(b * B, (b + 1) * B)
-                nc.scalar.activation(squares[:], centred[:, cols], ACT.Square, accum_out=sums[:, b : b + 1])
-            rstd = work.tile([B, W // B], F32, name="rstd")
-            nc.scalar.activation(
-                rstd[:, 0:blocks], sums[:, 0:blocks], ACT.Abs_reciprocal_sqrt, bias=eps[:], scale=1.0 / C
-            )
+            centred, turned_back = banks[p][:, 0:W], banks[p][:, W:BANK]
             normed = work.tile([B, W], F32, name="normed")
             nc.vector.tensor_tensor(
-                normed[:, 0:width].rearrange("p (b c) -> p b c", c=C),
+                normed[:].rearrange("p (b c) -> p b c", c=C),
                 centred.rearrange("p (b c) -> p b c", c=C),
-                rstd[:, 0:blocks].unsqueeze(2).to_broadcast([B, blocks, C]),
+                rstds[p][:].unsqueeze(2).to_broadcast([B, W // B, C]),
                 ALU.mult,
             )
-            for b in range(blocks):
-                cols = slice(b * B, (b + 1) * B)
+            for cols in blocks:
                 nc.tensor.transpose(turned_back[:, cols], normed[:, cols], identity[:])
             result = work.tile([C, W], F32, name="result")
-            nc.scalar.activation(result[:, 0:width], turned_back, ACT.Identity, bias=bias[:], scale=gain[:])
-            nc.sync.dma_start(out[:, start : start + width], result[:, 0:width])
+            nc.scalar.activation(result[:], turned_back, ACT.Identity, bias=bias[:], scale=gain[:])
+            nc.sync.dma_start(out[:, p * W : (p + 1) * W], result[:])

@@ -57,6 +57,8 @@ def tile_ternaryberttiny_kernel(tc, tok_emb, pos_emb, ln_gain, ln_bias, offs, ou
         make_identity(nc, identity[:])
         eps = held.tile([B, 1], F32, name="eps")
         nc.vector.memset(eps[:], EPS)
+        first_rstd = held.tile([B, 1], F32, name="first_rstd")
+        nc.scalar.activation(first_rstd[:], eps[:], ACT.Abs_reciprocal_sqrt)
         warm = held.tile([C, C], F32, name="warm")
         nc.vector.memset(warm[:], 0.0)
 

@@ -14,9 +14,12 @@ B = 128
 W = 2 * B
 BANK = 2 * W
 PIECES = N // W
-LOOK_UPS = [B] * 2 + [W] * (PIECES - 1)
 EPS = 1e-5
 WARM_UP = 7
+LOOK_AHEAD = 1
+SCALE_BEHIND = 3
+FINISH_BEHIND = 5
+SELF_SCALED = 2
 
 FLOPS = 8 * C * N
 
@@ -30,7 +33,7 @@ def tile_ternaryberttiny_kernel(tc, tok_emb, pos_emb, ln_gain, ln_bias, offs, ou
     ):
         offsets = held.tile([C, N // 16], U16, name="offsets")
         nc.sync.dma_start(offsets[:], offs)
-        early = LOOK_UPS[0]
+        early = B
         first_positions = held.tile([C, early], F32, name="first_positions")
         nc.sync.dma_start(first_positions[:], pos_emb[:, 0:early])
         table = held.tile([C, S], F32, name="table")
@@ -68,17 +71,24 @@ def tile_ternaryberttiny_kernel(tc, tok_emb, pos_emb, ln_gain, ln_bias, offs, ou
             nc.tensor.matmul(banks[PIECES - 1][:, 0:C], warm[:], warm[:], start=True, stop=True)
 
         embedded = held.tile([C, N], F32, name="embedded")
-        start = 0
-        for k, width in enumerate(LOOK_UPS):
+
+        def look_up(start, width, added):
             words = table[:].indirect(offsets[:, start // 16 : (start + width) // 16])
-            first = start % T
-            added = first_positions[:] if k == 0 else positions[:, first : first + width]
             nc.vector.tensor_tensor(embedded[:, start : start + width], words, added, ALU.add)
-            start += width
+
+        def look_up_piece(p):
+            first = p * W % T
+            if p == 0:
+                look_up(0, B, first_positions[:])
+                look_up(B, B, positions[:, B:W])
+            else:
+                look_up(p * W, W, positions[:, first : first + W])
 
         blocks = [slice(b * B, (b + 1) * B) for b in range(W // B)]
-        rstds = []
-        for p in range(PIECES):
+        rstds = [held.tile([B, W // B], F32, name=f"rstd{p}") for p in range(PIECES)]
+        norms = [held.tile([B, W], F32, name=f"norm{p}") for p in range(PIECES)]
+
+        def centre_and_sum(p):
             centred = banks[p][:, 0:W]
             for cols in blocks:
                 block = embedded[:, p * W + cols.start : p * W + cols.stop]
@@ -87,20 +97,40 @@ def tile_ternaryberttiny_kernel(tc, tok_emb, pos_emb, ln_gain, ln_bias, offs, ou
             for b, cols in enumerate(blocks):
                 squares = work.tile([B, C], F32, name="squares")
                 nc.scalar.activation(squares[:], centred[:, cols], ACT.Square, accum_out=sums[:, b : b + 1])
-            rstds.append(held.tile([B, W // B], F32, name=f"rstd{p}"))
             nc.scalar.activation(rstds[p][:], sums[:], ACT.Abs_reciprocal_sqrt, bias=eps[:], scale=1.0 / C)
 
-        for p in range(PIECES):
-            centred, turned_back = banks[p][:, 0:W], banks[p][:, W:BANK]
-            normed = work.tile([B, W], F32, name="normed")
-            nc.vector.tensor_tensor(
-                normed[:].rearrange("p (b c) -> p b c", c=C),
-                centred.rearrange("p (b c) -> p b c", c=C),
-                rstds[p][:].unsqueeze(2).to_broadcast([B, W // B, C]),
-                ALU.mult,
-            )
+        def scale(p):
+            centred = banks[p][:, 0:W]
+            if p < SELF_SCALED:
+                for b, cols in enumerate(blocks):
+                    nc.scalar.activation(norms[p][:, cols], centred[:, cols], ACT.Identity, scale=rstds[p][:, b : b + 1])
+            else:
+                nc.vector.tensor_tensor(
+                    norms[p][:].rearrange("p (b c) -> p b c", c=C),
+                    centred.rearrange("p (b c) -> p b c", c=C),
+                    rstds[p][:].unsqueeze(2).to_broadcast([B, W // B, C]),
+                    ALU.mult,
+                )
+
+        def finish(p):
+            turned_back = banks[p][:, W:BANK]
             for cols in blocks:
-                nc.tensor.transpose(turned_back[:, cols], normed[:, cols], identity[:])
+                nc.tensor.transpose(turned_back[:, cols], norms[p][:, cols], identity[:])
             result = work.tile([C, W], F32, name="result")
-            nc.scalar.activation(result[:], turned_back, ACT.Identity, bias=bias[:], scale=gain[:])
+            if p % 2 == 0:
+                nc.scalar.activation(result[:], turned_back, ACT.Identity, bias=bias[:], scale=gain[:])
+            else:
+                nc.vector.tensor_scalar(result[:], turned_back, gain[:], bias[:], ALU.mult, ALU.add)
             nc.sync.dma_start(out[:, p * W : (p + 1) * W], result[:])
+
+        for p in range(LOOK_AHEAD):
+            look_up_piece(p)
+        for step in range(PIECES + FINISH_BEHIND):
+            if step + LOOK_AHEAD < PIECES:
+                look_up_piece(step + LOOK_AHEAD)
+            if step < PIECES:
+                centre_and_sum(step)
+            if 0 <= step - SCALE_BEHIND < PIECES:
+                scale(step - SCALE_BEHIND)
+            if 0 <= step - FINISH_BEHIND < PIECES:
+                finish(step - FINISH_BEHIND)

@@ -37,9 +37,12 @@ def tile_ternaryberttiny_kernel(tc, tok_emb, pos_emb, ln_gain, ln_bias, offs, ou
         first_positions = held.tile([C, early], F32, name="first_positions")
         nc.sync.dma_start(first_positions[:], pos_emb[:, 0:early])
         table = held.tile([C, S], F32, name="table")
-        nc.scalar.dma_start(table[:], tok_emb)
+        ahead = (N // 16 * 2 + early * 4) // 4
+        split = (S - ahead) // 2
+        nc.sync.dma_start(table[:, 0:split], tok_emb[:, 0:split])
+        nc.scalar.dma_start(table[:, split:S], tok_emb[:, split:S])
         positions = held.tile([C, T], F32, name="positions")
-        nc.scalar.dma_start(positions[:], pos_emb)
+        nc.sync.dma_start(positions[:], pos_emb)
         gain = held.tile([C, 1], F32, name="gain")
         nc.sync.dma_start(gain[:], ln_gain)
         bias = held.tile([C, 1], F32, name="bias")

@@ -17,9 +17,9 @@ PIECES = N // W
 EPS = 1e-5
 WARM_UP = 7
 LOOK_AHEAD = 1
-SCALE_BEHIND = 3
-FINISH_BEHIND = 5
-SELF_SCALED = 2
+SCALE_BEHIND = 2
+FINISH_BEHIND = 4
+SCALED_BY_SCALAR = (0, 1, PIECES - 1)
 
 FLOPS = 8 * C * N
 
@@ -33,16 +33,14 @@ def tile_ternaryberttiny_kernel(tc, tok_emb, pos_emb, ln_gain, ln_bias, offs, ou
     ):
         offsets = held.tile([C, N // 16], U16, name="offsets")
         nc.sync.dma_start(offsets[:], offs)
-        early = B
-        first_positions = held.tile([C, early], F32, name="first_positions")
-        nc.sync.dma_start(first_positions[:], pos_emb[:, 0:early])
+        positions = held.tile([C, T], F32, name="positions")
+        nc.sync.dma_start(positions[:, 0:B], pos_emb[:, 0:B])
         table = held.tile([C, S], F32, name="table")
-        ahead = (N // 16 * 2 + early * 4) // 4
+        ahead = (N // 16 * 2 + B * 4) // 4
         split = (S - ahead) // 2
         nc.sync.dma_start(table[:, 0:split], tok_emb[:, 0:split])
         nc.scalar.dma_start(table[:, split:S], tok_emb[:, split:S])
-        positions = held.tile([C, T], F32, name="positions")
-        nc.sync.dma_start(positions[:], pos_emb)
+        nc.sync.dma_start(positions[:, B:T], pos_emb[:, B:T])
         gain = held.tile([C, 1], F32, name="gain")
         nc.sync.dma_start(gain[:], ln_gain)
         bias = held.tile([C, 1], F32, name="bias")
@@ -82,7 +80,7 @@ def tile_ternaryberttiny_kernel(tc, tok_emb, pos_emb, ln_gain, ln_bias, offs, ou
         def look_up_piece(p):
             first = p * W % T
             if p == 0:
-                look_up(0, B, first_positions[:])
+                look_up(0, B, positions[:, 0:B])
                 look_up(B, B, positions[:, B:W])
             else:
                 look_up(p * W, W, positions[:, first : first + W])
@@ -104,7 +102,7 @@ def tile_ternaryberttiny_kernel(tc, tok_emb, pos_emb, ln_gain, ln_bias, offs, ou
 
         def scale(p):
             centred = banks[p][:, 0:W]
-            if p < SELF_SCALED:
+            if p in SCALED_BY_SCALAR:
                 for b, cols in enumerate(blocks):
                     nc.scalar.activation(norms[p][:, cols], centred[:, cols], ACT.Identity, scale=rstds[p][:, b : b + 1])
             else:
@@ -120,10 +118,7 @@ def tile_ternaryberttiny_kernel(tc, tok_emb, pos_emb, ln_gain, ln_bias, offs, ou
             for cols in blocks:
                 nc.tensor.transpose(turned_back[:, cols], norms[p][:, cols], identity[:])
             result = work.tile([C, W], F32, name="result")
-            if p % 2 == 0:
-                nc.scalar.activation(result[:], turned_back, ACT.Identity, bias=bias[:], scale=gain[:])
-            else:
-                nc.vector.tensor_scalar(result[:], turned_back, gain[:], bias[:], ALU.mult, ALU.add)
+            nc.vector.tensor_scalar(result[:], turned_back, gain[:], bias[:], ALU.mult, ALU.add)
             nc.sync.dma_start(out[:, p * W : (p + 1) * W], result[:])
 
         for p in range(LOOK_AHEAD):

import concourse.mybir as mybir
from concourse.masks import make_identity

F32 = mybir.dt.float32
U16 = mybir.dt.uint16
ALU = mybir.AluOpType
ACT = mybir.ActivationFunctionType

C = 128
S = 1024
T = 512
N = 4 * T
B = 128
W = 2 * B
BANK = 2 * W
PIECES = N // W
EPS = 1e-5
WARM_UP = 7
LOOK_AHEAD = 1
SCALE_BEHIND = 2
FINISH_BEHIND = 4
SCALED_BY_SCALAR = (0, 1, PIECES - 1)

FLOPS = 8 * C * N


def tile_ternaryberttiny_kernel(tc, tok_emb, pos_emb, ln_gain, ln_bias, offs, out):
    nc = tc.nc
    with (
        tc.tile_pool(name="held", bufs=1) as held,
        tc.tile_pool(name="work", bufs=PIECES) as work,
        tc.psum_pool(name="psum", bufs=1) as psum,
    ):
        offsets = held.tile([C, N // 16], U16, name="offsets")
        nc.sync.dma_start(offsets[:], offs)
        positions = held.tile([C, T], F32, name="positions")
        nc.sync.dma_start(positions[:, 0:B], pos_emb[:, 0:B])
        table = held.tile([C, S], F32, name="table")
        ahead = (N // 16 * 2 + B * 4) // 4
        split = (S - ahead) // 2
        nc.sync.dma_start(table[:, 0:split], tok_emb[:, 0:split])
        nc.scalar.dma_start(table[:, split:S], tok_emb[:, split:S])
        nc.sync.dma_start(positions[:, B:T], pos_emb[:, B:T])
        gain = held.tile([C, 1], F32, name="gain")
        nc.sync.dma_start(gain[:], ln_gain)
        bias = held.tile([C, 1], F32, name="bias")
        nc.sync.dma_start(bias[:], ln_bias)

        centre_w = held.tile([C, C], F32, name="centre_w")
        nc.gpsimd.memset(centre_w[:], -1.0 / C)
        nc.gpsimd.affine_select(
            out=centre_w[:],
            in_=centre_w[:],
            pattern=[[-1, C]],
            compare_op=ALU.not_equal,
            fill=1.0 - 1.0 / C,
            base=0,
            channel_multiplier=1,
        )
        identity = held.tile([C, C], F32, name="identity")
        make_identity(nc, identity[:])
        eps = held.tile([B, 1], F32, name="eps")
        nc.vector.memset(eps[:], EPS)
        first_rstd = held.tile([B, 1], F32, name="first_rstd")
        nc.scalar.activation(first_rstd[:], eps[:], ACT.Abs_reciprocal_sqrt)
        warm = held.tile([C, C], F32, name="warm")
        nc.vector.memset(warm[:], 0.0)

        banks = [psum.tile([C, BANK], F32, name=f"bank{p}") for p in range(PIECES)]

        for i in range(WARM_UP):
            nc.tensor.matmul(banks[PIECES - 1][:, 0:C], warm[:], warm[:], start=True, stop=True)

        embedded = held.tile([C, N], F32, name="embedded")

        def look_up(start, width, added):
            words = table[:].indirect(offsets[:, start // 16 : (start + width) // 16])
            nc.vector.tensor_tensor(embedded[:, start : start + width], words, added, ALU.add)

        def look_up_piece(p):
            first = p * W % T
            if p == 0:
                look_up(0, B, positions[:, 0:B])
                look_up(B, B, positions[:, B:W])
            else:
                look_up(p * W, W, positions[:, first : first + W])

        blocks = [slice(b * B, (b + 1) * B) for b in range(W // B)]
        rstds = [held.tile([B, W // B], F32, name=f"rstd{p}") for p in range(PIECES)]
        norms = [held.tile([B, W], F32, name=f"norm{p}") for p in range(PIECES)]

        def centre_and_sum(p):
            centred = banks[p][:, 0:W]
            for cols in blocks:
                block = embedded[:, p * W + cols.start : p * W + cols.stop]
                nc.tensor.matmul(centred[:, cols], block, centre_w[:], start=True, stop=True)
            sums = work.tile([B, W // B], F32, name="sums")
            for b, cols in enumerate(blocks):
                squares = work.tile([B, C], F32, name="squares")
                nc.scalar.activation(squares[:], centred[:, cols], ACT.Square, accum_out=sums[:, b : b + 1])
            nc.scalar.activation(rstds[p][:], sums[:], ACT.Abs_reciprocal_sqrt, bias=eps[:], scale=1.0 / C)

        def scale(p):
            centred = banks[p][:, 0:W]
            if p in SCALED_BY_SCALAR:
                for b, cols in enumerate(blocks):
                    nc.scalar.activation(norms[p][:, cols], centred[:, cols], ACT.Identity, scale=rstds[p][:, b : b + 1])
            else:
                nc.vector.tensor_tensor(
                    norms[p][:].rearrange("p (b c) -> p b c", c=C),
                    centred.rearrange("p (b c) -> p b c", c=C),
                    rstds[p][:].unsqueeze(2).to_broadcast([B, W // B, C]),
                    ALU.mult,
                )

        def finish(p):
            turned_back = banks[p][:, W:BANK]
            for cols in blocks:
                nc.tensor.transpose(turned_back[:, cols], norms[p][:, cols], identity[:])
            result = work.tile([C, W], F32, name="result")
            nc.vector.tensor_scalar(result[:], turned_back, gain[:], bias[:], ALU.mult, ALU.add)
            nc.sync.dma_start(out[:, p * W : (p + 1) * W], result[:])

        for p in range(LOOK_AHEAD):
            look_up_piece(p)
        for step in range(PIECES + FINISH_BEHIND):
            if step + LOOK_AHEAD < PIECES:
                look_up_piece(step + LOOK_AHEAD)
            if step < PIECES:
                centre_and_sum(step)
            if 0 <= step - SCALE_BEHIND < PIECES:
                scale(step - SCALE_BEHIND)
            if 0 <= step - FINISH_BEHIND < PIECES:
                finish(step - FINISH_BEHIND)
